import numpy as np
import ml_dtypes


def mxq(x, axis, fmt="e4m3"):
    dtype, down = {"e4m3": (ml_dtypes.float8_e4m3fn, 7), "e5m2": (ml_dtypes.float8_e5m2, 14)}[fmt]
    v = np.moveaxis(np.asarray(x, np.float32).astype(ml_dtypes.bfloat16).astype(np.float64), axis, -1)
    blocks = v.reshape(v.shape[:-1] + (-1, 32))
    amax = np.abs(blocks).max(-1, keepdims=True)
    byte = np.maximum(np.where(amax > 0, np.frexp(amax)[1] - 1 + 127, 0) - down, 1)
    scale = np.exp2(byte - 127.0)
    codes = (blocks / scale).astype(np.float32).astype(dtype).astype(np.float64)
    return np.moveaxis((codes * scale).reshape(v.shape), -1, axis)


WIDE = False


def mx_kscale(k):
    if not WIDE:
        return np.ones(k)
    levels = np.array([10, -10, 5, -5, 0])
    a = np.random.permutation(np.resize(levels, k // 512 * 4)).reshape(k // 512, 4)
    idx = np.arange(k)
    return np.exp2(a[idx // 512, idx % 128 // 32])


BF16 = ml_dtypes.bfloat16


def bf(x):
    return np.asarray(x, np.float32).astype(BF16)


def f64(x):
    return np.asarray(x).astype(np.float64)


E2M1 = np.array([0.0, 0.5, 1.0, 1.5, 2.0, 3.0, 4.0, 6.0, -0.0, -0.5, -1.0, -1.5, -2.0, -3.0, -4.0, -6.0])


def pack_weight(w, fmt):
    k, n = w.shape
    w = f64(bf(w)).reshape(k // 32, 32, n)
    amax = np.abs(w).max(1)
    if fmt == "e4m3":
        byte = np.frexp(amax)[1] - 1 + 127 - 7
    else:
        mant, ex = np.frexp(amax / 6.0)
        byte = np.where(mant > 0.5, ex, ex - 1) + 127
    byte = np.clip(np.where(amax > 0, byte, 1), 1, 254)
    scaled = (w * np.exp2(127.0 - byte)[:, None, :]).reshape(k, n).astype(np.float32)
    by_word = np.ascontiguousarray(scaled.reshape(k // 512, 128, 4, n).transpose(0, 1, 3, 2))
    if fmt == "e4m3":
        words = by_word.astype(ml_dtypes.float8_e4m3fn).view(np.uint8)
    else:
        c = by_word.astype(ml_dtypes.float4_e2m1fn).view(np.uint8) & 0xF
        words = c[..., 0::2] | (c[..., 1::2] << 4)
    return np.ascontiguousarray(words), np.ascontiguousarray(byte.astype(np.uint8).reshape(k // 512, 16, n))


def unpack_weight(words, scales, fmt):
    g, p, n, _ = words.shape
    if fmt == "e4m3":
        vals = np.ascontiguousarray(words).view(ml_dtypes.float8_e4m3fn).astype(np.float64)
    else:
        nib = np.empty((g, p, n, 4), np.uint8)
        nib[..., 0::2] = words & 0xF
        nib[..., 1::2] = words >> 4
        vals = E2M1[nib]
    vals = vals * np.repeat(np.exp2(scales.astype(np.float64) - 127.0), 8, axis=1)[..., None]
    return vals.transpose(0, 1, 3, 2).reshape(g * 512, n)


E, LMAX, MMAX, CIN, COUT = 512, 4, 2, 512, 128
NS = [LMAX + 1 - m for m in range(MMAX + 1)]
NC = NS[0] + sum(2 * n for n in NS[1:])
FMT = "e4m3"


def setup_inputs():
    ss = [mx_kscale(n * CIN) for n in NS]
    sx = np.concatenate([ss[0].reshape(NS[0], CIN)] + [np.tile(ss[m].reshape(NS[m], CIN), (2, 1)) for m in range(1, MMAX + 1)], axis=0)
    x = np.random.standard_normal((E, NC, CIN)) * sx
    W0 = np.random.standard_normal((NS[0] * COUT, NS[0] * CIN)) / np.sqrt(NS[0] * CIN) / ss[0][None, :]
    b0 = np.random.standard_normal(NS[0] * COUT) * 0.3
    W1 = np.random.standard_normal((2 * NS[1] * COUT, NS[1] * CIN)) / (np.sqrt(2.0) * np.sqrt(NS[1] * CIN)) / ss[1][None, :]
    W2 = np.random.standard_normal((2 * NS[2] * COUT, NS[2] * CIN)) / (np.sqrt(2.0) * np.sqrt(NS[2] * CIN)) / ss[2][None, :]
    W0_words, W0_scales = pack_weight(np.ascontiguousarray(W0.T), FMT)
    W1_words, W1_scales = pack_weight(np.ascontiguousarray(W1.T), FMT)
    W2_words, W2_scales = pack_weight(np.ascontiguousarray(W2.T), FMT)
    return {"x": bf(x), "W0_words": W0_words, "W0_scales": W0_scales, "b0": bf(b0), "W1_words": W1_words, "W1_scales": W1_scales, "W2_words": W2_words, "W2_scales": W2_scales}


def reference(x, W0_words, W0_scales, b0, W1_words, W1_scales, W2_words, W2_scales):
    x = f64(x)
    WmT = [unpack_weight(W1_words, W1_scales, FMT), unpack_weight(W2_words, W2_scales, FMT)]
    outs = []
    x0 = x[:, :LMAX + 1].reshape(E, (LMAX + 1) * CIN)
    y0 = (mxq(x0, 1, "e4m3") @ unpack_weight(W0_words, W0_scales, FMT)) + f64(b0)
    outs.append(y0.reshape(E, LMAX + 1, COUT))
    offset = LMAX + 1
    for m in range(1, MMAX + 1):
        n = LMAX + 1 - m
        xm = x[:, offset:offset + 2 * n].reshape(E, 2, n * CIN)
        offset += 2 * n
        ym = mxq(xm, 2, "e4m3") @ WmT[m - 1]
        of = n * COUT
        x_r, x_i = ym[..., :of], ym[..., of:]
        pos = x_r[:, 0] - x_i[:, 1]
        neg = x_r[:, 1] + x_i[:, 0]
        outs.append(pos.reshape(E, n, COUT))
        outs.append(neg.reshape(E, n, COUT))
    return np.concatenate(outs, axis=1)

@@ -1,0 +1,216 @@
+from contextlib import ExitStack
+
+import concourse.mybir as mybir
+from concourse.masks import make_identity
+
+F32 = mybir.dt.float32
+BF16 = mybir.dt.bfloat16
+I32 = mybir.dt.int32
+U32 = mybir.dt.uint32
+U8 = mybir.dt.uint8
+FP8X4 = mybir.dt.float8_e4m3fn_x4
+
+P = 128
+EDGES = 512
+EDGE_TILES = EDGES // P
+LMAX = 4
+MMAX = 2
+CIN = 512
+COUT = 128
+WORDS = CIN // 2
+BANK = 512
+PLANES_PER_TILE = 4
+
+FLOPS = 2 * EDGES * (2560 * 640 + 2 * 2048 * 1024 + 2 * 1536 * 768)
+
+
+def order_shape(m):
+    degrees = LMAX + 1 - m
+    if m == 0:
+        return 0, degrees, degrees
+    first = LMAX + 1 + sum(2 * (LMAX + 1 - q) for q in range(1, m))
+    return first, degrees, 2 * degrees
+
+
+def column_chunks(width):
+    chunks = []
+    start = 0
+    for size in (512, 256, 128):
+        while width - start >= size:
+            chunks.append((start, size))
+            start += size
+    return chunks
+
+
+def tile_so2linear_kernel(
+    tc, x, W0_words, W0_scales, b0, W1_words, W1_scales, W2_words, W2_scales, out
+):
+    nc = tc.nc
+    given_words = {0: W0_words, 1: W1_words, 2: W2_words}
+    given_scales = {0: W0_scales, 1: W1_scales, 2: W2_scales}
+    units = [(m, et) for m in (2, 1, 0) for et in range(EDGE_TILES)]
+
+    with ExitStack() as ctx:
+        ctx.enter_context(tc.manual_schedule())
+        resident = ctx.enter_context(tc.tile_pool(name="resident", bufs=1))
+        grouped_pool = ctx.enter_context(tc.tile_pool(name="grouped", bufs=4))
+        codes_pool = ctx.enter_context(tc.tile_pool(name="codes", bufs=3))
+        part_pool = ctx.enter_context(tc.tile_pool(name="part", bufs=2))
+        turned_pool = ctx.enter_context(tc.psum_pool(name="turned", bufs=4))
+        acc_pool = ctx.enter_context(tc.psum_pool(name="acc", bufs=4))
+
+        identity = resident.tile([P, P], F32, name="identity")
+        make_identity(nc, identity[:])
+
+        x_tiles = {}
+        out_tiles = {}
+        for m, et in units:
+            components = order_shape(m)[2]
+            x_tiles[(m, et)] = resident.tile([P, components * CIN], BF16, name="x_%d_%d" % (m, et))
+            out_tiles[(m, et)] = resident.tile(
+                [P, components * COUT], F32, name="out_%d_%d" % (m, et)
+            )
+        w_words = {}
+        w_planes = {}
+        for m in range(MMAX + 1):
+            passes = given_words[m].shape[0]
+            n_cols = given_words[m].shape[2]
+            plane_tiles = (passes + PLANES_PER_TILE - 1) // PLANES_PER_TILE
+            w_words[m] = resident.tile([P, passes, n_cols], U32, name="w_words_%d" % m, align_bytes=64)
+            w_planes[m] = resident.tile(
+                [P, plane_tiles, n_cols], U8, name="w_planes_%d" % m, align_bytes=64
+            )
+            nc.vector.memset(w_planes[m][:].bitcast(I32), 0)
+        bias = resident.tile([P, (LMAX + 1) * COUT], BF16, name="bias")
+
+        def load_x(m, et):
+            first, degrees, components = order_shape(m)
+            nc.sync.dma_start(
+                out=x_tiles[(m, et)][:],
+                in_=x[et * P : (et + 1) * P, first : first + components, :].rearrange(
+                    "e c k -> e (c k)"
+                ),
+            )
+
+        def load_weight(m):
+            passes = given_words[m].shape[0]
+            for first_pass in range(0, passes, PLANES_PER_TILE):
+                together = min(PLANES_PER_TILE, passes - first_pass)
+                for quadrant in range(4):
+                    nc.sync.dma_start(
+                        out=w_planes[m][
+                            32 * quadrant : 32 * quadrant + 4 * together,
+                            first_pass // PLANES_PER_TILE,
+                            :,
+                        ].bitcast(I32),
+                        in_=given_scales[m][
+                            first_pass : first_pass + together, 4 * quadrant : 4 * quadrant + 4, :
+                        ].bitcast(I32),
+                    )
+            for g in range(passes):
+                nc.sync.dma_start(
+                    out=w_words[m][:, g, :].bitcast(I32),
+                    in_=given_words[m][g].rearrange("p n t -> p (n t)").bitcast(I32),
+                )
+
+        load_x(*units[0])
+        for i, (m, et) in enumerate(units):
+            if i + 1 < len(units):
+                load_x(*units[i + 1])
+            if et == 0:
+                load_weight(m)
+        nc.sync.dma_start(out=bias[:], in_=b0.partition_broadcast(P))
+
+        def quantise_unit(m, et):
+            components = order_shape(m)[2]
+            x_words = x_tiles[(m, et)][:].bitcast(F32)
+            codes = codes_pool.tile([P, components, P], U32, name="codes", align_bytes=64)
+            planes = codes_pool.tile([P, components, P], U8, name="planes", align_bytes=64)
+            for c0 in range(0, components, 2):
+                pair = min(2, components - c0)
+                turned = turned_pool.tile([P, 2, 2, P], F32, name="turned")
+                for c in range(pair):
+                    for u in range(2):
+                        nc.tensor.transpose(
+                            turned[:, c, u, :],
+                            x_words[:, (c0 + c) * WORDS + u : (c0 + c + 1) * WORDS : 2],
+                            identity[:],
+                        )
+                grouped = grouped_pool.tile([P, 2 * P * 4], BF16, name="grouped", align_bytes=64)
+                nc.scalar.copy(
+                    out=grouped[:, 0 : pair * P * 4]
+                    .bitcast(F32)
+                    .rearrange("p (c e u) -> p c e u", c=pair, u=2),
+                    in_=turned[:, 0:pair, :, :].rearrange("p c u e -> p c e u"),
+                )
+                nc.vector.quantize_mx(
+                    out=codes[:, c0 : c0 + pair, :].rearrange("p c e -> p (c e)").bitcast(FP8X4),
+                    scales=planes[:, c0 : c0 + pair, :].rearrange("p c e -> p (c e)"),
+                    in_=grouped[:, 0 : pair * P * 4],
+                )
+            return codes, planes
+
+        def accumulate(m, quantised, acc, width, terms):
+            codes, planes = quantised
+            for start, size in column_chunks(width):
+                for t, (c, g, col) in enumerate(terms):
+                    cols = slice(col + start, col + start + size)
+                    nc.tensor.matmul_mx(
+                        out=acc[:, start : start + size],
+                        lhsT=codes[:, c, :].bitcast(FP8X4),
+                        lhsT_scale=planes[:, c, :],
+                        rhs=w_words[m][:, g, cols].bitcast(FP8X4),
+                        rhs_scale=w_planes[m][
+                            4 * (g % PLANES_PER_TILE) : P, g // PLANES_PER_TILE, cols
+                        ],
+                        start=(t == 0),
+                        stop=(t == len(terms) - 1),
+                    )
+
+        def multiply_unit(m, et, quantised):
+            first, degrees, components = order_shape(m)
+            result = out_tiles[(m, et)]
+            half = degrees * COUT
+            if m == 0:
+                for col in range(0, half, BANK):
+                    width = min(BANK, half - col)
+                    acc = acc_pool.tile([P, BANK], F32, name="acc")
+                    accumulate(m, quantised, acc, width, [(g, g, col) for g in range(degrees)])
+                    nc.vector.tensor_add(
+                        out=result[:, col : col + width],
+                        in0=acc[:, 0:width],
+                        in1=bias[:, col : col + width],
+                    )
+            else:
+                real = [(g, g) for g in range(degrees)]
+                imag = [(degrees + g, g) for g in range(degrees)]
+                imag_wi = acc_pool.tile([P, BANK], F32, name="acc")
+                accumulate(m, quantised, imag_wi, half, [(c, g, half) for c, g in imag])
+                imag_wi_sb = part_pool.tile([P, BANK], F32, name="imag_wi_sb")
+                nc.scalar.copy(out=imag_wi_sb[:, 0:half], in_=imag_wi[:, 0:half])
+                real_wr = acc_pool.tile([P, BANK], F32, name="acc")
+                accumulate(m, quantised, real_wr, half, [(c, g, 0) for c, g in real])
+                nc.vector.tensor_sub(
+                    out=result[:, 0:half], in0=real_wr[:, 0:half], in1=imag_wi_sb[:, 0:half]
+                )
+                cross = acc_pool.tile([P, BANK], F32, name="acc")
+                accumulate(
+                    m,
+                    quantised,
+                    cross,
+                    half,
+                    [(c, g, 0) for c, g in imag] + [(c, g, half) for c, g in real],
+                )
+                nc.vector.tensor_copy(out=result[:, half : 2 * half], in_=cross[:, 0:half])
+            nc.sync.dma_start(
+                out=out[et * P : (et + 1) * P, first : first + components, :].rearrange(
+                    "e c o -> e (c o)"
+                ),
+                in_=result[:],
+            )
+
+        quantised = quantise_unit(*units[0])
+        for i, (m, et) in enumerate(units):
+            following = quantise_unit(*units[i + 1]) if i + 1 < len(units) else None
+            multiply_unit(m, et, quantised)
+            quantised = following

@@ -17,7 +17,6 @@ LMAX = 4
 MMAX = 2
 CIN = 512
 COUT = 128
-WORDS = CIN // 2
 BANK = 512
 PLANES_PER_TILE = 4
 
@@ -53,6 +52,7 @@ def tile_so2linear_kernel(
     with ExitStack() as ctx:
         ctx.enter_context(tc.manual_schedule())
         resident = ctx.enter_context(tc.tile_pool(name="resident", bufs=1))
+        sorted_pool = ctx.enter_context(tc.tile_pool(name="sorted", bufs=2))
         grouped_pool = ctx.enter_context(tc.tile_pool(name="grouped", bufs=4))
         codes_pool = ctx.enter_context(tc.tile_pool(name="codes", bufs=3))
         part_pool = ctx.enter_context(tc.tile_pool(name="part", bufs=2))
@@ -121,9 +121,19 @@ def tile_so2linear_kernel(
                 load_weight(m)
         nc.sync.dma_start(out=bias[:], in_=b0.partition_broadcast(P))
 
-        def quantise_unit(m, et):
+        def sort_unit(m, et):
             components = order_shape(m)[2]
-            x_words = x_tiles[(m, et)][:].bitcast(F32)
+            sorted_words = sorted_pool.tile([P, components, 2, P], F32, name="sorted_words")
+            nc.vector.tensor_copy(
+                out=sorted_words[:],
+                in_=x_tiles[(m, et)][:]
+                .bitcast(F32)
+                .rearrange("p (c w u) -> p c u w", c=components, u=2),
+            )
+            return sorted_words
+
+        def quantise_unit(m, et, sorted_words):
+            components = order_shape(m)[2]
             codes = codes_pool.tile([P, components, P], U32, name="codes", align_bytes=64)
             planes = codes_pool.tile([P, components, P], U8, name="planes", align_bytes=64)
             for c0 in range(0, components, 2):
@@ -133,7 +143,7 @@ def tile_so2linear_kernel(
                     for u in range(2):
                         nc.tensor.transpose(
                             turned[:, c, u, :],
-                            x_words[:, (c0 + c) * WORDS + u : (c0 + c + 1) * WORDS : 2],
+                            sorted_words[:, c0 + c, u, :],
                             identity[:],
                         )
                 grouped = grouped_pool.tile([P, 2 * P * 4], BF16, name="grouped", align_bytes=64)
@@ -209,8 +219,13 @@ def tile_so2linear_kernel(
                 in_=result[:],
             )
 
-        quantised = quantise_unit(*units[0])
+        sorted_units = [sort_unit(*units[0]), sort_unit(*units[1])]
+        quantised = quantise_unit(*units[0], sorted_units[0])
         for i, (m, et) in enumerate(units):
-            following = quantise_unit(*units[i + 1]) if i + 1 < len(units) else None
+            if i + 2 < len(units):
+                sorted_units.append(sort_unit(*units[i + 2]))
+            following = None
+            if i + 1 < len(units):
+                following = quantise_unit(*units[i + 1], sorted_units[i + 1])
             multiply_unit(m, et, quantised)
             quantised = following

@@ -177,8 +177,17 @@ def tile_so2linear_kernel(
                         stop=(t == len(terms) - 1),
                     )
 
+        def store_columns(m, et, col, width):
+            first = order_shape(m)[0]
+            nc.sync.dma_start(
+                out=out[
+                    et * P : (et + 1) * P, first + col // COUT : first + (col + width) // COUT, :
+                ].rearrange("e c o -> e (c o)"),
+                in_=out_tiles[(m, et)][:, col : col + width],
+            )
+
         def multiply_unit(m, et, quantised):
-            first, degrees, components = order_shape(m)
+            degrees = order_shape(m)[1]
             result = out_tiles[(m, et)]
             half = degrees * COUT
             if m == 0:
@@ -191,6 +200,7 @@ def tile_so2linear_kernel(
                         in0=acc[:, 0:width],
                         in1=bias[:, col : col + width],
                     )
+                    store_columns(m, et, col, width)
             else:
                 real = [(g, g) for g in range(degrees)]
                 imag = [(degrees + g, g) for g in range(degrees)]
@@ -203,6 +213,7 @@ def tile_so2linear_kernel(
                 nc.vector.tensor_sub(
                     out=result[:, 0:half], in0=real_wr[:, 0:half], in1=imag_wi_sb[:, 0:half]
                 )
+                store_columns(m, et, 0, half)
                 cross = acc_pool.tile([P, BANK], F32, name="acc")
                 accumulate(
                     m,
@@ -212,12 +223,7 @@ def tile_so2linear_kernel(
                     [(c, g, 0) for c, g in imag] + [(c, g, half) for c, g in real],
                 )
                 nc.vector.tensor_copy(out=result[:, half : 2 * half], in_=cross[:, 0:half])
-            nc.sync.dma_start(
-                out=out[et * P : (et + 1) * P, first : first + components, :].rearrange(
-                    "e c o -> e (c o)"
-                ),
-                in_=result[:],
-            )
+                store_columns(m, et, half, half)
 
         sorted_units = [sort_unit(*units[0]), sort_unit(*units[1])]
         quantised = quantise_unit(*units[0], sorted_units[0])

@@ -123,12 +123,12 @@ def tile_so2linear_kernel(
 
         def sort_unit(m, et):
             components = order_shape(m)[2]
-            sorted_words = sorted_pool.tile([P, components, 2, P], F32, name="sorted_words")
+            sorted_words = sorted_pool.tile([P, 2, components * P], F32, name="sorted_words")
             nc.vector.tensor_copy(
                 out=sorted_words[:],
                 in_=x_tiles[(m, et)][:]
                 .bitcast(F32)
-                .rearrange("p (c w u) -> p c u w", c=components, u=2),
+                .rearrange("p (w u) -> p u w", u=2),
             )
             return sorted_words
 
@@ -143,7 +143,7 @@ def tile_so2linear_kernel(
                     for u in range(2):
                         nc.tensor.transpose(
                             turned[:, c, u, :],
-                            sorted_words[:, c0 + c, u, :],
+                            sorted_words[:, u, (c0 + c) * P : (c0 + c + 1) * P],
                             identity[:],
                         )
                 grouped = grouped_pool.tile([P, 2 * P * 4], BF16, name="grouped", align_bytes=64)

@@ -18,6 +18,7 @@ MMAX = 2
 CIN = 512
 COUT = 128
 BANK = 512
+FIRST_PIECES = 3
 PLANES_PER_TILE = 4
 
 FLOPS = 2 * EDGES * (2560 * 640 + 2 * 2048 * 1024 + 2 * 1536 * 768)
@@ -29,16 +30,6 @@ def order_shape(m):
         return 0, degrees, degrees
     first = LMAX + 1 + sum(2 * (LMAX + 1 - q) for q in range(1, m))
     return first, degrees, 2 * degrees
-
-
-def column_chunks(width):
-    chunks = []
-    start = 0
-    for size in (512, 256, 128):
-        while width - start >= size:
-            chunks.append((start, size))
-            start += size
-    return chunks
 
 
 def tile_so2linear_kernel(
@@ -53,6 +44,7 @@ def tile_so2linear_kernel(
         ctx.enter_context(tc.manual_schedule())
         resident = ctx.enter_context(tc.tile_pool(name="resident", bufs=1))
         sorted_pool = ctx.enter_context(tc.tile_pool(name="sorted", bufs=2))
+        pieces_pool = ctx.enter_context(tc.tile_pool(name="pieces", bufs=FIRST_PIECES))
         grouped_pool = ctx.enter_context(tc.tile_pool(name="grouped", bufs=4))
         codes_pool = ctx.enter_context(tc.tile_pool(name="codes", bufs=3))
         part_pool = ctx.enter_context(tc.tile_pool(name="part", bufs=2))
@@ -72,7 +64,7 @@ def tile_so2linear_kernel(
             )
         w_words = {}
         w_planes = {}
-        for m in range(MMAX + 1):
+        for m in (2, 1, 0):
             passes = given_words[m].shape[0]
             n_cols = given_words[m].shape[2]
             plane_tiles = (passes + PLANES_PER_TILE - 1) // PLANES_PER_TILE
@@ -83,14 +75,16 @@ def tile_so2linear_kernel(
             nc.vector.memset(w_planes[m][:].bitcast(I32), 0)
         bias = resident.tile([P, (LMAX + 1) * COUT], BF16, name="bias")
 
-        def load_x(m, et):
+        def load_x(m, et, pieces=1):
             first, degrees, components = order_shape(m)
-            nc.sync.dma_start(
-                out=x_tiles[(m, et)][:],
-                in_=x[et * P : (et + 1) * P, first : first + components, :].rearrange(
-                    "e c k -> e (c k)"
-                ),
-            )
+            size = components // pieces
+            for c in range(0, components, size):
+                nc.sync.dma_start(
+                    out=x_tiles[(m, et)][:, c * CIN : (c + size) * CIN],
+                    in_=x[et * P : (et + 1) * P, first + c : first + c + size, :].rearrange(
+                        "e c k -> e (c k)"
+                    ),
+                )
 
         def load_weight(m):
             passes = given_words[m].shape[0]
@@ -113,7 +107,7 @@ def tile_so2linear_kernel(
                     in_=given_words[m][g].rearrange("p n t -> p (n t)").bitcast(I32),
                 )
 
-        load_x(*units[0])
+        load_x(*units[0], pieces=FIRST_PIECES)
         for i, (m, et) in enumerate(units):
             if i + 1 < len(units):
                 load_x(*units[i + 1])
@@ -121,31 +115,29 @@ def tile_so2linear_kernel(
                 load_weight(m)
         nc.sync.dma_start(out=bias[:], in_=b0.partition_broadcast(P))
 
-        def sort_unit(m, et):
-            components = order_shape(m)[2]
-            sorted_words = sorted_pool.tile([P, 2, components * P], F32, name="sorted_words")
-            nc.vector.tensor_copy(
-                out=sorted_words[:],
-                in_=x_tiles[(m, et)][:]
-                .bitcast(F32)
-                .rearrange("p (w u) -> p u w", u=2),
-            )
-            return sorted_words
+        def sort_unit(i, pieces=1):
+            m, et = units[i]
+            size = order_shape(m)[2] // pieces
+            words = []
+            for piece in range(pieces):
+                pool = sorted_pool if pieces == 1 else pieces_pool
+                sorted_words = pool.tile([P, 2, size * P], F32, name="sorted_words")
+                nc.vector.tensor_copy(
+                    out=sorted_words[:],
+                    in_=x_tiles[(m, et)][:, piece * size * CIN : (piece + 1) * size * CIN]
+                    .bitcast(F32)
+                    .rearrange("p (w u) -> p u w", u=2),
+                )
+                for c in range(size):
+                    words.append([sorted_words[:, u, c * P : (c + 1) * P] for u in range(2)])
+            return words
 
-        def quantise_unit(m, et, sorted_words):
-            components = order_shape(m)[2]
+        def transpose_unit(i):
+            components = order_shape(units[i][0])[2]
             codes = codes_pool.tile([P, components, P], U32, name="codes", align_bytes=64)
             planes = codes_pool.tile([P, components, P], U8, name="planes", align_bytes=64)
-            for c0 in range(0, components, 2):
-                pair = min(2, components - c0)
-                turned = turned_pool.tile([P, 2, 2, P], F32, name="turned")
-                for c in range(pair):
-                    for u in range(2):
-                        nc.tensor.transpose(
-                            turned[:, c, u, :],
-                            sorted_words[:, u, (c0 + c) * P : (c0 + c + 1) * P],
-                            identity[:],
-                        )
+
+            def regroup_and_quantise(turned, c0, pair):
                 grouped = grouped_pool.tile([P, 2 * P * 4], BF16, name="grouped", align_bytes=64)
                 nc.scalar.copy(
                     out=grouped[:, 0 : pair * P * 4]
@@ -158,24 +150,42 @@ def tile_so2linear_kernel(
                     scales=planes[:, c0 : c0 + pair, :].rearrange("p c e -> p (c e)"),
                     in_=grouped[:, 0 : pair * P * 4],
                 )
-            return codes, planes
 
-        def accumulate(m, quantised, acc, width, terms):
-            codes, planes = quantised
-            for start, size in column_chunks(width):
-                for t, (c, g, col) in enumerate(terms):
-                    cols = slice(col + start, col + start + size)
-                    nc.tensor.matmul_mx(
-                        out=acc[:, start : start + size],
-                        lhsT=codes[:, c, :].bitcast(FP8X4),
-                        lhsT_scale=planes[:, c, :],
-                        rhs=w_words[m][:, g, cols].bitcast(FP8X4),
-                        rhs_scale=w_planes[m][
-                            4 * (g % PLANES_PER_TILE) : P, g // PLANES_PER_TILE, cols
-                        ],
-                        start=(t == 0),
-                        stop=(t == len(terms) - 1),
-                    )
+            steps = []
+            for c0 in range(0, components, 2):
+                pair = min(2, components - c0)
+                turned = turned_pool.tile([P, 2, 2, P], F32, name="turned")
+                for c in range(pair):
+                    for u in range(2):
+                        nc.tensor.transpose(
+                            turned[:, c, u, :], sorted_units[i][c0 + c][u], identity[:]
+                        )
+                steps.append(
+                    lambda turned=turned, c0=c0, pair=pair: regroup_and_quantise(turned, c0, pair)
+                )
+            quantised[i] = [(codes[:, c, :], planes[:, c, :]) for c in range(components)]
+            return steps
+
+        def prepare(i):
+            for step in transpose_unit(i):
+                step()
+
+        def add_pass(m, acc, width, term, parts, start, stop):
+            c, g, col = term
+            cols = slice(col, col + width)
+            nc.tensor.matmul_mx(
+                out=acc[:, 0:width],
+                lhsT=parts[c][0].bitcast(FP8X4),
+                lhsT_scale=parts[c][1],
+                rhs=w_words[m][:, g, cols].bitcast(FP8X4),
+                rhs_scale=w_planes[m][4 * (g % PLANES_PER_TILE) : P, g // PLANES_PER_TILE, cols],
+                start=start,
+                stop=stop,
+            )
+
+        def add_passes(m, acc, width, terms, parts):
+            for t, term in enumerate(terms):
+                add_pass(m, acc, width, term, parts, t == 0, t == len(terms) - 1)
 
         def store_columns(m, et, col, width):
             first = order_shape(m)[0]
@@ -186,52 +196,84 @@ def tile_so2linear_kernel(
                 in_=out_tiles[(m, et)][:, col : col + width],
             )
 
-        def multiply_unit(m, et, quantised):
+        def multiply_unit(i, halfway):
+            m, et = units[i]
+            parts = quantised[i]
             degrees = order_shape(m)[1]
             result = out_tiles[(m, et)]
             half = degrees * COUT
+
             if m == 0:
-                for col in range(0, half, BANK):
-                    width = min(BANK, half - col)
+                for col, width in ((0, BANK), (BANK, half - BANK)):
                     acc = acc_pool.tile([P, BANK], F32, name="acc")
-                    accumulate(m, quantised, acc, width, [(g, g, col) for g in range(degrees)])
+                    add_passes(m, acc, width, [(g, g, col) for g in range(degrees)], parts)
                     nc.vector.tensor_add(
                         out=result[:, col : col + width],
                         in0=acc[:, 0:width],
                         in1=bias[:, col : col + width],
                     )
                     store_columns(m, et, col, width)
+            elif m == 2:
+                over = BANK - half
+                rest = half - over
+                for c0 in (0, degrees):
+                    wide = acc_pool.tile([P, BANK], F32, name="acc")
+                    narrow = acc_pool.tile([P, BANK], F32, name="acc")
+                    for g in range(degrees):
+                        flags = (g == 0, g == degrees - 1)
+                        add_pass(m, wide, BANK, (c0 + g, g, 0), parts, *flags)
+                        add_pass(m, narrow, rest, (c0 + g, g, BANK), parts, *flags)
+                    if c0 == 0:
+                        real = part_pool.tile([P, 2 * half], F32, name="real")
+                        nc.scalar.copy(out=real[:, 0:BANK], in_=wide[:])
+                        nc.scalar.copy(out=real[:, BANK:], in_=narrow[:, 0:rest])
+                        if halfway is not None:
+                            halfway()
+                nc.vector.tensor_add(
+                    out=result[:, half:], in0=wide[:, 0:half], in1=real[:, half:]
+                )
+                store_columns(m, et, half, half)
+                nc.vector.tensor_sub(
+                    out=result[:, 0:over], in0=real[:, 0:over], in1=wide[:, half:]
+                )
+                nc.vector.tensor_sub(
+                    out=result[:, over:half], in0=real[:, over:half], in1=narrow[:, 0:rest]
+                )
+                store_columns(m, et, 0, half)
             else:
                 real = [(g, g) for g in range(degrees)]
                 imag = [(degrees + g, g) for g in range(degrees)]
                 imag_wi = acc_pool.tile([P, BANK], F32, name="acc")
-                accumulate(m, quantised, imag_wi, half, [(c, g, half) for c, g in imag])
+                add_passes(m, imag_wi, half, [(c, g, half) for c, g in imag], parts)
                 imag_wi_sb = part_pool.tile([P, BANK], F32, name="imag_wi_sb")
-                nc.scalar.copy(out=imag_wi_sb[:, 0:half], in_=imag_wi[:, 0:half])
+                nc.scalar.copy(out=imag_wi_sb[:], in_=imag_wi[:])
                 real_wr = acc_pool.tile([P, BANK], F32, name="acc")
-                accumulate(m, quantised, real_wr, half, [(c, g, 0) for c, g in real])
-                nc.vector.tensor_sub(
-                    out=result[:, 0:half], in0=real_wr[:, 0:half], in1=imag_wi_sb[:, 0:half]
-                )
+                add_passes(m, real_wr, half, [(c, g, 0) for c, g in real], parts)
+                nc.vector.tensor_sub(out=result[:, 0:half], in0=real_wr[:], in1=imag_wi_sb[:])
                 store_columns(m, et, 0, half)
                 cross = acc_pool.tile([P, BANK], F32, name="acc")
-                accumulate(
+                add_passes(
                     m,
-                    quantised,
                     cross,
                     half,
                     [(c, g, 0) for c, g in imag] + [(c, g, half) for c, g in real],
+                    parts,
                 )
-                nc.vector.tensor_copy(out=result[:, half : 2 * half], in_=cross[:, 0:half])
+                nc.scalar.copy(out=result[:, half : 2 * half], in_=cross[:])
                 store_columns(m, et, half, half)
 
-        sorted_units = [sort_unit(*units[0]), sort_unit(*units[1])]
-        quantised = quantise_unit(*units[0], sorted_units[0])
-        for i, (m, et) in enumerate(units):
-            if i + 2 < len(units):
-                sorted_units.append(sort_unit(*units[i + 2]))
-            following = None
-            if i + 1 < len(units):
-                following = quantise_unit(*units[i + 1], sorted_units[i + 1])
-            multiply_unit(m, et, quantised)
-            quantised = following
+        quantised = {}
+        sorted_units = {0: sort_unit(0, pieces=FIRST_PIECES)}
+        steps = transpose_unit(0)
+        steps[0]()
+        sorted_units[1] = sort_unit(1)
+        for step in steps[1:]:
+            step()
+        prepare(1)
+        sorted_units[2] = sort_unit(2)
+        for i in range(len(units)):
+            if 0 < i and i + 2 < len(units):
+                sorted_units[i + 2] = sort_unit(i + 2)
+            if 1 < i and i + 1 < len(units):
+                prepare(i + 1)
+            multiply_unit(i, (lambda: prepare(2)) if i == 1 else None)

@@ -18,7 +18,9 @@ MMAX = 2
 CIN = 512
 COUT = 128
 BANK = 512
-FIRST_PIECES = 3
+PIECES = {0: 3}
+TURNED_BANKS = 4
+BORROWED_BANKS = 2
 PLANES_PER_TILE = 4
 
 FLOPS = 2 * EDGES * (2560 * 640 + 2 * 2048 * 1024 + 2 * 1536 * 768)
@@ -44,11 +46,11 @@ def tile_so2linear_kernel(
         ctx.enter_context(tc.manual_schedule())
         resident = ctx.enter_context(tc.tile_pool(name="resident", bufs=1))
         sorted_pool = ctx.enter_context(tc.tile_pool(name="sorted", bufs=2))
-        pieces_pool = ctx.enter_context(tc.tile_pool(name="pieces", bufs=FIRST_PIECES))
+        pieces_pool = ctx.enter_context(tc.tile_pool(name="pieces", bufs=max(PIECES.values())))
         grouped_pool = ctx.enter_context(tc.tile_pool(name="grouped", bufs=4))
         codes_pool = ctx.enter_context(tc.tile_pool(name="codes", bufs=3))
         part_pool = ctx.enter_context(tc.tile_pool(name="part", bufs=2))
-        turned_pool = ctx.enter_context(tc.psum_pool(name="turned", bufs=4))
+        turned_pool = ctx.enter_context(tc.psum_pool(name="turned", bufs=TURNED_BANKS))
         acc_pool = ctx.enter_context(tc.psum_pool(name="acc", bufs=4))
 
         identity = resident.tile([P, P], F32, name="identity")
@@ -75,9 +77,10 @@ def tile_so2linear_kernel(
             nc.vector.memset(w_planes[m][:].bitcast(I32), 0)
         bias = resident.tile([P, (LMAX + 1) * COUT], BF16, name="bias")
 
-        def load_x(m, et, pieces=1):
+        def load_x(i):
+            m, et = units[i]
             first, degrees, components = order_shape(m)
-            size = components // pieces
+            size = components // PIECES.get(i, 1)
             for c in range(0, components, size):
                 nc.sync.dma_start(
                     out=x_tiles[(m, et)][:, c * CIN : (c + size) * CIN],
@@ -107,16 +110,17 @@ def tile_so2linear_kernel(
                     in_=given_words[m][g].rearrange("p n t -> p (n t)").bitcast(I32),
                 )
 
-        load_x(*units[0], pieces=FIRST_PIECES)
+        load_x(0)
         for i, (m, et) in enumerate(units):
             if i + 1 < len(units):
-                load_x(*units[i + 1])
+                load_x(i + 1)
             if et == 0:
                 load_weight(m)
         nc.sync.dma_start(out=bias[:], in_=b0.partition_broadcast(P))
 
-        def sort_unit(i, pieces=1):
+        def sort_unit(i):
             m, et = units[i]
+            pieces = PIECES.get(i, 1)
             size = order_shape(m)[2] // pieces
             words = []
             for piece in range(pieces):
@@ -132,10 +136,10 @@ def tile_so2linear_kernel(
                     words.append([sorted_words[:, u, c * P : (c + 1) * P] for u in range(2)])
             return words
 
-        def transpose_unit(i):
-            components = order_shape(units[i][0])[2]
-            codes = codes_pool.tile([P, components, P], U32, name="codes", align_bytes=64)
-            planes = codes_pool.tile([P, components, P], U8, name="planes", align_bytes=64)
+        def transpose_units(*run):
+            words = [pair for i in run for pair in sorted_units[i]]
+            codes = codes_pool.tile([P, len(words), P], U32, name="codes", align_bytes=64)
+            planes = codes_pool.tile([P, len(words), P], U8, name="planes", align_bytes=64)
 
             def regroup_and_quantise(turned, c0, pair):
                 grouped = grouped_pool.tile([P, 2 * P * 4], BF16, name="grouped", align_bytes=64)
@@ -152,22 +156,28 @@ def tile_so2linear_kernel(
                 )
 
             steps = []
-            for c0 in range(0, components, 2):
-                pair = min(2, components - c0)
-                turned = turned_pool.tile([P, 2, 2, P], F32, name="turned")
+            for c0 in range(0, len(words), 2):
+                pair = min(2, len(words) - c0)
+                if len(steps) == TURNED_BANKS + BORROWED_BANKS:
+                    steps.pop(0)()
+                if TURNED_BANKS <= c0 // 2 < TURNED_BANKS + BORROWED_BANKS:
+                    turned = acc_pool.tile([P, 2, 2, P], F32, name="acc")
+                else:
+                    turned = turned_pool.tile([P, 2, 2, P], F32, name="turned")
                 for c in range(pair):
                     for u in range(2):
-                        nc.tensor.transpose(
-                            turned[:, c, u, :], sorted_units[i][c0 + c][u], identity[:]
-                        )
+                        nc.tensor.transpose(turned[:, c, u, :], words[c0 + c][u], identity[:])
                 steps.append(
                     lambda turned=turned, c0=c0, pair=pair: regroup_and_quantise(turned, c0, pair)
                 )
-            quantised[i] = [(codes[:, c, :], planes[:, c, :]) for c in range(components)]
+            operands = [(codes[:, c, :], planes[:, c, :]) for c in range(len(words))]
+            size = len(words) // len(run)
+            for n, i in enumerate(run):
+                quantised[i] = operands[n * size : (n + 1) * size]
             return steps
 
-        def prepare(i):
-            for step in transpose_unit(i):
+        def prepare(*run):
+            for step in transpose_units(*run):
                 step()
 
         def add_pass(m, acc, width, term, parts, start, stop):
@@ -263,17 +273,23 @@ def tile_so2linear_kernel(
                 store_columns(m, et, half, half)
 
         quantised = {}
-        sorted_units = {0: sort_unit(0, pieces=FIRST_PIECES)}
-        steps = transpose_unit(0)
+        sorted_units = {0: sort_unit(0)}
+        steps = transpose_units(0)
         steps[0]()
         sorted_units[1] = sort_unit(1)
         for step in steps[1:]:
             step()
         prepare(1)
         sorted_units[2] = sort_unit(2)
+        runs = {i: (i + 1,) for i in range(2, 5)}
+        for i in range(5, len(units) - 1, 2):
+            runs[i] = (i + 1, i + 2)
         for i in range(len(units)):
-            if 0 < i and i + 2 < len(units):
+            if 0 < i < 4:
                 sorted_units[i + 2] = sort_unit(i + 2)
-            if 1 < i and i + 1 < len(units):
-                prepare(i + 1)
+            if i in runs:
+                prepare(*runs[i])
+            if i % 2 == 0 and 4 <= i < len(units) - 2:
+                sorted_units[i + 2] = sort_unit(i + 2)
+                sorted_units[i + 3] = sort_unit(i + 3)
             multiply_unit(i, (lambda: prepare(2)) if i == 1 else None)

@@ -21,7 +21,7 @@ BANK = 512
 PIECES = {0: 3}
 TURNED_BANKS = 4
 BORROWED_BANKS = 2
-PLANES_PER_TILE = 4
+PLANES_PER_TILE = {0: 4, 1: 4, 2: 2}
 
 FLOPS = 2 * EDGES * (2560 * 640 + 2 * 2048 * 1024 + 2 * 1536 * 768)
 
@@ -69,7 +69,7 @@ def tile_so2linear_kernel(
         for m in (2, 1, 0):
             passes = given_words[m].shape[0]
             n_cols = given_words[m].shape[2]
-            plane_tiles = (passes + PLANES_PER_TILE - 1) // PLANES_PER_TILE
+            plane_tiles = (passes + PLANES_PER_TILE[m] - 1) // PLANES_PER_TILE[m]
             w_words[m] = resident.tile([P, passes, n_cols], U32, name="w_words_%d" % m, align_bytes=64)
             w_planes[m] = resident.tile(
                 [P, plane_tiles, n_cols], U8, name="w_planes_%d" % m, align_bytes=64
@@ -89,33 +89,37 @@ def tile_so2linear_kernel(
                     ),
                 )
 
-        def load_weight(m):
-            passes = given_words[m].shape[0]
-            for first_pass in range(0, passes, PLANES_PER_TILE):
-                together = min(PLANES_PER_TILE, passes - first_pass)
-                for quadrant in range(4):
-                    nc.sync.dma_start(
-                        out=w_planes[m][
-                            32 * quadrant : 32 * quadrant + 4 * together,
-                            first_pass // PLANES_PER_TILE,
-                            :,
-                        ].bitcast(I32),
-                        in_=given_scales[m][
-                            first_pass : first_pass + together, 4 * quadrant : 4 * quadrant + 4, :
-                        ].bitcast(I32),
-                    )
-            for g in range(passes):
+        def load_scales(m, n):
+            first = PLANES_PER_TILE[m] * n
+            given = given_scales[m][first : min(first + PLANES_PER_TILE[m], given_scales[m].shape[0])]
+            for quadrant in range(4):
                 nc.sync.dma_start(
-                    out=w_words[m][:, g, :].bitcast(I32),
-                    in_=given_words[m][g].rearrange("p n t -> p (n t)").bitcast(I32),
+                    out=w_planes[m][
+                        32 * quadrant : 32 * quadrant + 4 * given.shape[0], n, :
+                    ].bitcast(I32),
+                    in_=given[:, 4 * quadrant : 4 * quadrant + 4, :].bitcast(I32),
                 )
 
+        def load_words(m, g):
+            nc.sync.dma_start(
+                out=w_words[m][:, g, :].bitcast(I32),
+                in_=given_words[m][g].rearrange("p n t -> p (n t)").bitcast(I32),
+            )
+
         load_x(0)
+        load_x(1)
+        load_scales(2, 0)
+        for g in range(w_words[2].shape[1]):
+            load_words(2, g)
+        load_scales(2, 1)
         for i, (m, et) in enumerate(units):
-            if i + 1 < len(units):
+            if 1 < i + 1 < len(units):
                 load_x(i + 1)
-            if et == 0:
-                load_weight(m)
+            if et == 0 and m < 2:
+                for n in range(w_planes[m].shape[1]):
+                    load_scales(m, n)
+                for g in range(w_words[m].shape[1]):
+                    load_words(m, g)
         nc.sync.dma_start(out=bias[:], in_=b0.partition_broadcast(P))
 
         def sort_unit(i):
@@ -183,12 +187,13 @@ def tile_so2linear_kernel(
         def add_pass(m, acc, width, term, parts, start, stop):
             c, g, col = term
             cols = slice(col, col + width)
+            per_tile = PLANES_PER_TILE[m]
             nc.tensor.matmul_mx(
                 out=acc[:, 0:width],
                 lhsT=parts[c][0].bitcast(FP8X4),
                 lhsT_scale=parts[c][1],
                 rhs=w_words[m][:, g, cols].bitcast(FP8X4),
-                rhs_scale=w_planes[m][4 * (g % PLANES_PER_TILE) : P, g // PLANES_PER_TILE, cols],
+                rhs_scale=w_planes[m][4 * (g % per_tile) : P, g // per_tile, cols],
                 start=start,
                 stop=stop,
             )
@@ -226,14 +231,20 @@ def tile_so2linear_kernel(
             elif m == 2:
                 over = BANK - half
                 rest = half - over
-                for c0 in (0, degrees):
-                    wide = acc_pool.tile([P, BANK], F32, name="acc")
-                    narrow = acc_pool.tile([P, BANK], F32, name="acc")
-                    for g in range(degrees):
-                        flags = (g == 0, g == degrees - 1)
-                        add_pass(m, wide, BANK, (c0 + g, g, 0), parts, *flags)
-                        add_pass(m, narrow, rest, (c0 + g, g, BANK), parts, *flags)
-                    if c0 == 0:
+                order = [(c0, g) for c0 in (0, degrees) for g in range(degrees)]
+                if i == 0:
+                    order = sorted(order, key=lambda term: term[1] + (1.5 if term[0] else 0))
+                accs = {}
+                for c0, g in order:
+                    if g == 0:
+                        wide = acc_pool.tile([P, BANK], F32, name="acc")
+                        narrow = acc_pool.tile([P, BANK], F32, name="acc")
+                        accs[c0] = (wide, narrow)
+                    wide, narrow = accs[c0]
+                    flags = (g == 0, g == degrees - 1)
+                    add_pass(m, wide, BANK, (c0 + g, g, 0), parts, *flags)
+                    add_pass(m, narrow, rest, (c0 + g, g, BANK), parts, *flags)
+                    if (c0, g) == (0, degrees - 1):
                         real = part_pool.tile([P, 2 * half], F32, name="real")
                         nc.scalar.copy(out=real[:, 0:BANK], in_=wide[:])
                         nc.scalar.copy(out=real[:, BANK:], in_=narrow[:, 0:rest])

from contextlib import ExitStack

import concourse.mybir as mybir
from concourse.masks import make_identity

F32 = mybir.dt.float32
BF16 = mybir.dt.bfloat16
I32 = mybir.dt.int32
U32 = mybir.dt.uint32
U8 = mybir.dt.uint8
FP8X4 = mybir.dt.float8_e4m3fn_x4

P = 128
EDGES = 512
EDGE_TILES = EDGES // P
LMAX = 4
MMAX = 2
CIN = 512
COUT = 128
BANK = 512
PIECES = {0: 3}
TURNED_BANKS = 4
BORROWED_BANKS = 2
PLANES_PER_TILE = {0: 4, 1: 4, 2: 2}

FLOPS = 2 * EDGES * (2560 * 640 + 2 * 2048 * 1024 + 2 * 1536 * 768)


def order_shape(m):
    degrees = LMAX + 1 - m
    if m == 0:
        return 0, degrees, degrees
    first = LMAX + 1 + sum(2 * (LMAX + 1 - q) for q in range(1, m))
    return first, degrees, 2 * degrees


def tile_so2linear_kernel(
    tc, x, W0_words, W0_scales, b0, W1_words, W1_scales, W2_words, W2_scales, out
):
    nc = tc.nc
    given_words = {0: W0_words, 1: W1_words, 2: W2_words}
    given_scales = {0: W0_scales, 1: W1_scales, 2: W2_scales}
    units = [(m, et) for m in (2, 1, 0) for et in range(EDGE_TILES)]

    with ExitStack() as ctx:
        ctx.enter_context(tc.manual_schedule())
        resident = ctx.enter_context(tc.tile_pool(name="resident", bufs=1))
        sorted_pool = ctx.enter_context(tc.tile_pool(name="sorted", bufs=2))
        pieces_pool = ctx.enter_context(tc.tile_pool(name="pieces", bufs=max(PIECES.values())))
        grouped_pool = ctx.enter_context(tc.tile_pool(name="grouped", bufs=4))
        codes_pool = ctx.enter_context(tc.tile_pool(name="codes", bufs=3))
        part_pool = ctx.enter_context(tc.tile_pool(name="part", bufs=2))
        turned_pool = ctx.enter_context(tc.psum_pool(name="turned", bufs=TURNED_BANKS))
        acc_pool = ctx.enter_context(tc.psum_pool(name="acc", bufs=4))

        identity = resident.tile([P, P], F32, name="identity")
        make_identity(nc, identity[:])

        x_tiles = {}
        out_tiles = {}
        for m, et in units:
            components = order_shape(m)[2]
            x_tiles[(m, et)] = resident.tile([P, components * CIN], BF16, name="x_%d_%d" % (m, et))
            out_tiles[(m, et)] = resident.tile(
                [P, components * COUT], F32, name="out_%d_%d" % (m, et)
            )
        w_words = {}
        w_planes = {}
        for m in (2, 1, 0):
            passes = given_words[m].shape[0]
            n_cols = given_words[m].shape[2]
            plane_tiles = (passes + PLANES_PER_TILE[m] - 1) // PLANES_PER_TILE[m]
            w_words[m] = resident.tile([P, passes, n_cols], U32, name="w_words_%d" % m, align_bytes=64)
            w_planes[m] = resident.tile(
                [P, plane_tiles, n_cols], U8, name="w_planes_%d" % m, align_bytes=64
            )
            nc.vector.memset(w_planes[m][:].bitcast(I32), 0)
        bias = resident.tile([P, (LMAX + 1) * COUT], BF16, name="bias")

        def load_x(i):
            m, et = units[i]
            first, degrees, components = order_shape(m)
            size = components // PIECES.get(i, 1)
            for c in range(0, components, size):
                nc.sync.dma_start(
                    out=x_tiles[(m, et)][:, c * CIN : (c + size) * CIN],
                    in_=x[et * P : (et + 1) * P, first + c : first + c + size, :].rearrange(
                        "e c k -> e (c k)"
                    ),
                )

        def load_scales(m, n):
            first = PLANES_PER_TILE[m] * n
            given = given_scales[m][first : min(first + PLANES_PER_TILE[m], given_scales[m].shape[0])]
            for quadrant in range(4):
                nc.sync.dma_start(
                    out=w_planes[m][
                        32 * quadrant : 32 * quadrant + 4 * given.shape[0], n, :
                    ].bitcast(I32),
                    in_=given[:, 4 * quadrant : 4 * quadrant + 4, :].bitcast(I32),
                )

        def load_words(m, g):
            nc.sync.dma_start(
                out=w_words[m][:, g, :].bitcast(I32),
                in_=given_words[m][g].rearrange("p n t -> p (n t)").bitcast(I32),
            )

        load_x(0)
        load_x(1)
        load_scales(2, 0)
        for g in range(w_words[2].shape[1]):
            load_words(2, g)
        load_scales(2, 1)
        for i, (m, et) in enumerate(units):
            if 1 < i + 1 < len(units):
                load_x(i + 1)
            if et == 0 and m < 2:
                for n in range(w_planes[m].shape[1]):
                    load_scales(m, n)
                for g in range(w_words[m].shape[1]):
                    load_words(m, g)
        nc.sync.dma_start(out=bias[:], in_=b0.partition_broadcast(P))

        def sort_unit(i):
            m, et = units[i]
            pieces = PIECES.get(i, 1)
            size = order_shape(m)[2] // pieces
            words = []
            for piece in range(pieces):
                pool = sorted_pool if pieces == 1 else pieces_pool
                sorted_words = pool.tile([P, 2, size * P], F32, name="sorted_words")
                nc.vector.tensor_copy(
                    out=sorted_words[:],
                    in_=x_tiles[(m, et)][:, piece * size * CIN : (piece + 1) * size * CIN]
                    .bitcast(F32)
                    .rearrange("p (w u) -> p u w", u=2),
                )
                for c in range(size):
                    words.append([sorted_words[:, u, c * P : (c + 1) * P] for u in range(2)])
            return words

        def transpose_units(*run):
            words = [pair for i in run for pair in sorted_units[i]]
            codes = codes_pool.tile([P, len(words), P], U32, name="codes", align_bytes=64)
            planes = codes_pool.tile([P, len(words), P], U8, name="planes", align_bytes=64)

            def regroup_and_quantise(turned, c0, pair):
                grouped = grouped_pool.tile([P, 2 * P * 4], BF16, name="grouped", align_bytes=64)
                nc.scalar.copy(
                    out=grouped[:, 0 : pair * P * 4]
                    .bitcast(F32)
                    .rearrange("p (c e u) -> p c e u", c=pair, u=2),
                    in_=turned[:, 0:pair, :, :].rearrange("p c u e -> p c e u"),
                )
                nc.vector.quantize_mx(
                    out=codes[:, c0 : c0 + pair, :].rearrange("p c e -> p (c e)").bitcast(FP8X4),
                    scales=planes[:, c0 : c0 + pair, :].rearrange("p c e -> p (c e)"),
                    in_=grouped[:, 0 : pair * P * 4],
                )

            steps = []
            for c0 in range(0, len(words), 2):
                pair = min(2, len(words) - c0)
                if len(steps) == TURNED_BANKS + BORROWED_BANKS:
                    steps.pop(0)()
                if TURNED_BANKS <= c0 // 2 < TURNED_BANKS + BORROWED_BANKS:
                    turned = acc_pool.tile([P, 2, 2, P], F32, name="acc")
                else:
                    turned = turned_pool.tile([P, 2, 2, P], F32, name="turned")
                for c in range(pair):
                    for u in range(2):
                        nc.tensor.transpose(turned[:, c, u, :], words[c0 + c][u], identity[:])
                steps.append(
                    lambda turned=turned, c0=c0, pair=pair: regroup_and_quantise(turned, c0, pair)
                )
            operands = [(codes[:, c, :], planes[:, c, :]) for c in range(len(words))]
            size = len(words) // len(run)
            for n, i in enumerate(run):
                quantised[i] = operands[n * size : (n + 1) * size]
            return steps

        def prepare(*run):
            for step in transpose_units(*run):
                step()

        def add_pass(m, acc, width, term, parts, start, stop):
            c, g, col = term
            cols = slice(col, col + width)
            per_tile = PLANES_PER_TILE[m]
            nc.tensor.matmul_mx(
                out=acc[:, 0:width],
                lhsT=parts[c][0].bitcast(FP8X4),
                lhsT_scale=parts[c][1],
                rhs=w_words[m][:, g, cols].bitcast(FP8X4),
                rhs_scale=w_planes[m][4 * (g % per_tile) : P, g // per_tile, cols],
                start=start,
                stop=stop,
            )

        def add_passes(m, acc, width, terms, parts):
            for t, term in enumerate(terms):
                add_pass(m, acc, width, term, parts, t == 0, t == len(terms) - 1)

        def store_columns(m, et, col, width):
            first = order_shape(m)[0]
            nc.sync.dma_start(
                out=out[
                    et * P : (et + 1) * P, first + col // COUT : first + (col + width) // COUT, :
                ].rearrange("e c o -> e (c o)"),
                in_=out_tiles[(m, et)][:, col : col + width],
            )

        def multiply_unit(i, halfway):
            m, et = units[i]
            parts = quantised[i]
            degrees = order_shape(m)[1]
            result = out_tiles[(m, et)]
            half = degrees * COUT

            if m == 0:
                for col, width in ((0, BANK), (BANK, half - BANK)):
                    acc = acc_pool.tile([P, BANK], F32, name="acc")
                    add_passes(m, acc, width, [(g, g, col) for g in range(degrees)], parts)
                    nc.vector.tensor_add(
                        out=result[:, col : col + width],
                        in0=acc[:, 0:width],
                        in1=bias[:, col : col + width],
                    )
                    store_columns(m, et, col, width)
            elif m == 2:
                over = BANK - half
                rest = half - over
                order = [(c0, g) for c0 in (0, degrees) for g in range(degrees)]
                if i == 0:
                    order = sorted(order, key=lambda term: term[1] + (1.5 if term[0] else 0))
                accs = {}
                for c0, g in order:
                    if g == 0:
                        wide = acc_pool.tile([P, BANK], F32, name="acc")
                        narrow = acc_pool.tile([P, BANK], F32, name="acc")
                        accs[c0] = (wide, narrow)
                    wide, narrow = accs[c0]
                    flags = (g == 0, g == degrees - 1)
                    add_pass(m, wide, BANK, (c0 + g, g, 0), parts, *flags)
                    add_pass(m, narrow, rest, (c0 + g, g, BANK), parts, *flags)
                    if (c0, g) == (0, degrees - 1):
                        real = part_pool.tile([P, 2 * half], F32, name="real")
                        nc.scalar.copy(out=real[:, 0:BANK], in_=wide[:])
                        nc.scalar.copy(out=real[:, BANK:], in_=narrow[:, 0:rest])
                        if halfway is not None:
                            halfway()
                nc.vector.tensor_add(
                    out=result[:, half:], in0=wide[:, 0:half], in1=real[:, half:]
                )
                store_columns(m, et, half, half)
                nc.vector.tensor_sub(
                    out=result[:, 0:over], in0=real[:, 0:over], in1=wide[:, half:]
                )
                nc.vector.tensor_sub(
                    out=result[:, over:half], in0=real[:, over:half], in1=narrow[:, 0:rest]
                )
                store_columns(m, et, 0, half)
            else:
                real = [(g, g) for g in range(degrees)]
                imag = [(degrees + g, g) for g in range(degrees)]
                imag_wi = acc_pool.tile([P, BANK], F32, name="acc")
                add_passes(m, imag_wi, half, [(c, g, half) for c, g in imag], parts)
                imag_wi_sb = part_pool.tile([P, BANK], F32, name="imag_wi_sb")
                nc.scalar.copy(out=imag_wi_sb[:], in_=imag_wi[:])
                real_wr = acc_pool.tile([P, BANK], F32, name="acc")
                add_passes(m, real_wr, half, [(c, g, 0) for c, g in real], parts)
                nc.vector.tensor_sub(out=result[:, 0:half], in0=real_wr[:], in1=imag_wi_sb[:])
                store_columns(m, et, 0, half)
                cross = acc_pool.tile([P, BANK], F32, name="acc")
                add_passes(
                    m,
                    cross,
                    half,
                    [(c, g, 0) for c, g in imag] + [(c, g, half) for c, g in real],
                    parts,
                )
                nc.scalar.copy(out=result[:, half : 2 * half], in_=cross[:])
                store_columns(m, et, half, half)

        quantised = {}
        sorted_units = {0: sort_unit(0)}
        steps = transpose_units(0)
        steps[0]()
        sorted_units[1] = sort_unit(1)
        for step in steps[1:]:
            step()
        prepare(1)
        sorted_units[2] = sort_unit(2)
        runs = {i: (i + 1,) for i in range(2, 5)}
        for i in range(5, len(units) - 1, 2):
            runs[i] = (i + 1, i + 2)
        for i in range(len(units)):
            if 0 < i < 4:
                sorted_units[i + 2] = sort_unit(i + 2)
            if i in runs:
                prepare(*runs[i])
            if i % 2 == 0 and 4 <= i < len(units) - 2:
                sorted_units[i + 2] = sort_unit(i + 2)
                sorted_units[i + 3] = sort_unit(i + 3)
            multiply_unit(i, (lambda: prepare(2)) if i == 1 else None)
